import numpy as np
import ml_dtypes


def mxq(x, axis, fmt="e4m3"):
    dtype, down = {"e4m3": (ml_dtypes.float8_e4m3fn, 7), "e5m2": (ml_dtypes.float8_e5m2, 14)}[fmt]
    v = np.moveaxis(np.asarray(x, np.float32).astype(ml_dtypes.bfloat16).astype(np.float64), axis, -1)
    blocks = v.reshape(v.shape[:-1] + (-1, 32))
    amax = np.abs(blocks).max(-1, keepdims=True)
    byte = np.maximum(np.where(amax > 0, np.frexp(amax)[1] - 1 + 127, 0) - down, 1)
    scale = np.exp2(byte - 127.0)
    codes = (blocks / scale).astype(np.float32).astype(dtype).astype(np.float64)
    return np.moveaxis((codes * scale).reshape(v.shape), -1, axis)


WIDE = False


def mx_kscale(k):
    if not WIDE:
        return np.ones(k)
    levels = np.array([10, -10, 5, -5, 0])
    a = np.random.permutation(np.resize(levels, k // 512 * 4)).reshape(k // 512, 4)
    idx = np.arange(k)
    return np.exp2(a[idx // 512, idx % 128 // 32])


BF16 = ml_dtypes.bfloat16


def bf(x):
    return np.asarray(x, np.float32).astype(BF16)


def f64(x):
    return np.asarray(x).astype(np.float64)


B, IN, H, NS, SS, CS, NA = 128, 256, 1024, 4, 8, 128, 3
NC = NS * CS


def setup_inputs():
    s = mx_kscale(H)
    return {
        "h": bf(np.tanh(np.random.standard_normal((B, H))) * s),
        "act_logits": bf(np.random.standard_normal((B, NS * NA)) * 1.5),
        "stacks": bf(np.random.standard_normal((B, NS, SS, CS)) * 1.5),
        "W_push": bf(np.random.standard_normal((NC, H)) * 5.0 / np.sqrt(H) / s),
        "b_push": bf(np.random.standard_normal(NC) * 0.7),
    }


def reference(h, act_logits, stacks, W_push, b_push):
    st = f64(stacks)
    push = ((mxq(f64(h), 1, "e4m3") @ mxq(f64(W_push), 1, "e4m3").T) + f64(b_push)).reshape(B, NS, CS)
    lg = f64(act_logits)
    e = np.exp(lg - lg.max(-1, keepdims=True))
    act = (e / e.sum(-1, keepdims=True)).reshape(B, NS, NA)
    pa, po, no = act[..., 0][..., None], act[..., 1][..., None], act[..., 2][..., None]
    top_new = pa * push + po * st[:, :, 1, :] + no * st[:, :, 0, :]
    zeros_tail = np.zeros((B, NS, 1, CS))
    pop_rest = np.concatenate([st[:, :, 2:, :], zeros_tail], axis=2)
    rest = (pa[:, :, :, None] * st[:, :, :-1, :]
            + po[:, :, :, None] * pop_rest
            + no[:, :, :, None] * st[:, :, 1:, :])
    return np.concatenate([top_new[:, :, None, :], rest], axis=2)

@@ -1,0 +1,153 @@
+from contextlib import ExitStack
+
+import concourse.mybir as mybir
+from concourse.masks import make_identity
+
+F32 = mybir.dt.float32
+BF16 = mybir.dt.bfloat16
+U32 = mybir.dt.uint32
+U8 = mybir.dt.uint8
+FP8X4 = mybir.dt.float8_e4m3fn_x4
+ACT = mybir.ActivationFunctionType
+ALU = mybir.AluOpType
+AX = mybir.AxisListType
+
+P = 128
+H = 1024
+NS = 4
+SS = 8
+CS = 128
+NA = 3
+NC = NS * CS
+PACK = 4
+K_PASS = P * PACK
+PASSES = H // K_PASS
+HALVES = 2
+
+FLOPS = 2 * P * H * NC
+
+
+def transpose_rows(nc, bank, rows, identity):
+    words = rows.bitcast(F32)
+    for g in range(PASSES):
+        for u in range(HALVES):
+            first = (g * HALVES + u) * P
+            nc.tensor.transpose(bank[:, g, u, :], words[:, first : first + P], identity)
+
+
+def tile_stackrnncore_pa_s_kernel(tc, h, act_logits, stacks, W_push, b_push, out):
+    nc = tc.nc
+    with ExitStack() as ctx:
+        keep = ctx.enter_context(tc.tile_pool(name="keep", bufs=1))
+        psum = ctx.enter_context(tc.psum_pool(name="psum", bufs=1))
+
+        logits = keep.tile([P, NS * NA], BF16)
+        nc.scalar.dma_start(out=logits[:], in_=act_logits)
+        h_rows = keep.tile([P, H], BF16)
+        nc.sync.dma_start(out=h_rows[:], in_=h)
+        old = keep.tile([P, NS, SS, CS], BF16)
+        nc.sync.dma_start(out=old[:, 0], in_=stacks[:, 0])
+        w_rows = []
+        for n in range(NS):
+            w_rows_n = keep.tile([P, H], BF16, name="w_rows%d" % n)
+            nc.sync.dma_start(out=w_rows_n[:], in_=W_push[n * CS : (n + 1) * CS, :])
+            w_rows.append(w_rows_n)
+        for n in range(1, NS):
+            nc.sync.dma_start(out=old[:, n], in_=stacks[:, n])
+
+        identity = keep.tile([P, P], F32)
+        make_identity(nc, identity[:])
+        bias = keep.tile([P, NC], BF16)
+        nc.gpsimd.dma_start(out=bias[:], in_=b_push.partition_broadcast(P))
+
+        zero = keep.tile([P, 1], F32)
+        nc.vector.memset(zero[:], 0.0)
+        one = keep.tile([P, 1], F32)
+        nc.scalar.activation(out=one[:], in_=zero[:], func=ACT.Exp)
+
+        neg_max = keep.tile([P, 1], F32)
+        nc.vector.reduce_max(out=neg_max[:], in_=logits[:], axis=AX.X, negate=True)
+        expd = keep.tile([P, NS * NA], F32)
+        exp_sum = keep.tile([P, 1], F32)
+        nc.scalar.activation(
+            out=expd[:], in_=logits[:], func=ACT.Exp, bias=neg_max[:], accum_out=exp_sum[:]
+        )
+        inv_sum = keep.tile([P, 1], F32)
+        nc.vector.reciprocal(out=inv_sum[:], in_=exp_sum[:])
+        act = keep.tile([P, NS * NA], F32)
+        nc.vector.tensor_scalar_mul(out=act[:], in0=expd[:], scalar1=inv_sum[:])
+
+        h_bank = psum.tile([P, PASSES, HALVES, P], F32)
+        transpose_rows(nc, h_bank, h_rows[:], identity[:])
+        h_grouped = keep.tile([P, PASSES * P * PACK], BF16, align_bytes=64)
+        nc.vector.tensor_copy(
+            out=h_grouped[:].bitcast(F32).rearrange("p (g r u) -> p g r u", g=PASSES, u=HALVES),
+            in_=h_bank[:].rearrange("p g u r -> p g r u"),
+        )
+        h_codes = keep.tile([P, PASSES * P], U32, align_bytes=64)
+        h_scales = keep.tile([P, PASSES * P], U8, align_bytes=64)
+        nc.vector.quantize_mx(out=h_codes[:].bitcast(FP8X4), scales=h_scales[:], in_=h_grouped[:])
+
+        w_grouped = keep.tile([P, PASSES * NC * PACK], BF16, align_bytes=64)
+        w_grouped_words = w_grouped[:].bitcast(F32).rearrange(
+            "p (g c u) -> p g c u", g=PASSES, u=HALVES
+        )
+        for n in range(NS):
+            w_bank = psum.tile([P, PASSES, HALVES, P], F32, name="w_bank%d" % n)
+            transpose_rows(nc, w_bank, w_rows[n][:], identity[:])
+            nc.scalar.copy(
+                out=w_grouped_words[:, :, n * CS : (n + 1) * CS, :],
+                in_=w_bank[:].rearrange("p g u c -> p g c u"),
+            )
+        w_codes = keep.tile([P, PASSES * NC], U32, align_bytes=64)
+        w_scales = keep.tile([P, PASSES * NC], U8, align_bytes=64)
+        nc.vector.quantize_mx(out=w_codes[:].bitcast(FP8X4), scales=w_scales[:], in_=w_grouped[:])
+
+        push = psum.tile([P, NC], F32)
+        for g in range(PASSES):
+            nc.tensor.matmul_mx(
+                out=push[:],
+                lhsT=h_codes[:, g * P : (g + 1) * P].bitcast(FP8X4),
+                lhsT_scale=h_scales[:, g * P : (g + 1) * P],
+                rhs=w_codes[:, g * NC : (g + 1) * NC].bitcast(FP8X4),
+                rhs_scale=w_scales[:, g * NC : (g + 1) * NC],
+                start=(g == 0),
+                stop=(g == PASSES - 1),
+            )
+
+        new = keep.tile([P, NS, SS, CS], F32)
+        for n in range(NS):
+            pa = act[:, n * NA + 0 : n * NA + 1]
+            po = act[:, n * NA + 1 : n * NA + 2]
+            no = act[:, n * NA + 2 : n * NA + 3]
+            nc.scalar.activation(out=new[:, n], in_=old[:, n], func=ACT.Copy, scale=no)
+            nc.vector.scalar_tensor_tensor(
+                out=new[:, n, 1:SS],
+                in0=old[:, n, 0 : SS - 1],
+                scalar=pa,
+                in1=new[:, n, 1:SS],
+                op0=ALU.mult,
+                op1=ALU.add,
+            )
+            nc.vector.scalar_tensor_tensor(
+                out=new[:, n, 0 : SS - 1],
+                in0=old[:, n, 1:SS],
+                scalar=po,
+                in1=new[:, n, 0 : SS - 1],
+                op0=ALU.mult,
+                op1=ALU.add,
+            )
+            nc.sync.dma_start(out=out[:, n, 1:SS, :], in_=new[:, n, 1:SS, :])
+
+        pushed = keep.tile([P, NC], F32)
+        nc.vector.tensor_tensor(out=pushed[:], in0=push[:], in1=bias[:], op=ALU.add)
+        for n in range(NS):
+            nc.vector.scalar_tensor_tensor(
+                out=new[:, n, 0, :],
+                in0=pushed[:, n * CS : (n + 1) * CS],
+                scalar=act[:, n * NA : n * NA + 1],
+                in1=new[:, n, 0, :],
+                op0=ALU.mult,
+                op1=ALU.add,
+            )
+        nc.sync.dma_start(out=out[:, :, 0, :], in_=new[:, :, 0, :])

@@ -16,23 +16,15 @@ P = 128
 H = 1024
 NS = 4
 SS = 8
+HALF = SS // 2
 CS = 128
 NA = 3
-NC = NS * CS
 PACK = 4
 K_PASS = P * PACK
 PASSES = H // K_PASS
-HALVES = 2
+PAIRS = 2
 
-FLOPS = 2 * P * H * NC
-
-
-def transpose_rows(nc, bank, rows, identity):
-    words = rows.bitcast(F32)
-    for g in range(PASSES):
-        for u in range(HALVES):
-            first = (g * HALVES + u) * P
-            nc.tensor.transpose(bank[:, g, u, :], words[:, first : first + P], identity)
+FLOPS = 2 * P * H * NS * CS
 
 
 def tile_stackrnncore_pa_s_kernel(tc, h, act_logits, stacks, W_push, b_push, out):
@@ -40,25 +32,27 @@ def tile_stackrnncore_pa_s_kernel(tc, h, act_logits, stacks, W_push, b_push, out
     with ExitStack() as ctx:
         keep = ctx.enter_context(tc.tile_pool(name="keep", bufs=1))
         psum = ctx.enter_context(tc.psum_pool(name="psum", bufs=1))
+        ctx.enter_context(tc.manual_schedule())
 
         logits = keep.tile([P, NS * NA], BF16)
         nc.scalar.dma_start(out=logits[:], in_=act_logits)
-        h_rows = keep.tile([P, H], BF16)
-        nc.sync.dma_start(out=h_rows[:], in_=h)
+        bias_col = keep.tile([P, NS], BF16)
+        with nc.allow_non_contiguous_dma(reason="512 single elements, once"):
+            nc.scalar.dma_start(out=bias_col[:], in_=b_push.rearrange("(n c) -> c n", c=CS))
+
         old = keep.tile([P, NS, SS, CS], BF16)
+        h_rows = keep.tile([P, H], BF16)
+        w_rows = [keep.tile([P, H], BF16, name="w_rows%d" % n) for n in range(NS)]
         nc.sync.dma_start(out=old[:, 0], in_=stacks[:, 0])
-        w_rows = []
+        nc.sync.dma_start(out=old[:, 1], in_=stacks[:, 1])
+        nc.sync.dma_start(out=h_rows[:], in_=h)
         for n in range(NS):
-            w_rows_n = keep.tile([P, H], BF16, name="w_rows%d" % n)
-            nc.sync.dma_start(out=w_rows_n[:], in_=W_push[n * CS : (n + 1) * CS, :])
-            w_rows.append(w_rows_n)
-        for n in range(1, NS):
-            nc.sync.dma_start(out=old[:, n], in_=stacks[:, n])
+            nc.sync.dma_start(out=w_rows[n][:], in_=W_push[n * CS : (n + 1) * CS, :])
+        nc.sync.dma_start(out=old[:, 2], in_=stacks[:, 2])
+        nc.sync.dma_start(out=old[:, 3], in_=stacks[:, 3])
 
         identity = keep.tile([P, P], F32)
         make_identity(nc, identity[:])
-        bias = keep.tile([P, NC], BF16)
-        nc.gpsimd.dma_start(out=bias[:], in_=b_push.partition_broadcast(P))
 
         zero = keep.tile([P, 1], F32)
         nc.vector.memset(zero[:], 0.0)
@@ -74,78 +68,106 @@ def tile_stackrnncore_pa_s_kernel(tc, h, act_logits, stacks, W_push, b_push, out
         )
         inv_sum = keep.tile([P, 1], F32)
         nc.vector.reciprocal(out=inv_sum[:], in_=exp_sum[:])
-        act = keep.tile([P, NS * NA], F32)
-        nc.vector.tensor_scalar_mul(out=act[:], in0=expd[:], scalar1=inv_sum[:])
-
-        h_bank = psum.tile([P, PASSES, HALVES, P], F32)
-        transpose_rows(nc, h_bank, h_rows[:], identity[:])
-        h_grouped = keep.tile([P, PASSES * P * PACK], BF16, align_bytes=64)
-        nc.vector.tensor_copy(
-            out=h_grouped[:].bitcast(F32).rearrange("p (g r u) -> p g r u", g=PASSES, u=HALVES),
-            in_=h_bank[:].rearrange("p g u r -> p g r u"),
+        act = keep.tile([P, NS, NA], F32)
+        nc.vector.tensor_scalar_mul(
+            out=act[:].rearrange("p n a -> p (n a)"), in0=expd[:], scalar1=inv_sum[:]
         )
-        h_codes = keep.tile([P, PASSES * P], U32, align_bytes=64)
-        h_scales = keep.tile([P, PASSES * P], U8, align_bytes=64)
-        nc.vector.quantize_mx(out=h_codes[:].bitcast(FP8X4), scales=h_scales[:], in_=h_grouped[:])
-
-        w_grouped = keep.tile([P, PASSES * NC * PACK], BF16, align_bytes=64)
-        w_grouped_words = w_grouped[:].bitcast(F32).rearrange(
-            "p (g c u) -> p g c u", g=PASSES, u=HALVES
-        )
-        for n in range(NS):
-            w_bank = psum.tile([P, PASSES, HALVES, P], F32, name="w_bank%d" % n)
-            transpose_rows(nc, w_bank, w_rows[n][:], identity[:])
-            nc.scalar.copy(
-                out=w_grouped_words[:, :, n * CS : (n + 1) * CS, :],
-                in_=w_bank[:].rearrange("p g u c -> p g c u"),
-            )
-        w_codes = keep.tile([P, PASSES * NC], U32, align_bytes=64)
-        w_scales = keep.tile([P, PASSES * NC], U8, align_bytes=64)
-        nc.vector.quantize_mx(out=w_codes[:].bitcast(FP8X4), scales=w_scales[:], in_=w_grouped[:])
-
-        push = psum.tile([P, NC], F32)
-        for g in range(PASSES):
-            nc.tensor.matmul_mx(
-                out=push[:],
-                lhsT=h_codes[:, g * P : (g + 1) * P].bitcast(FP8X4),
-                lhsT_scale=h_scales[:, g * P : (g + 1) * P],
-                rhs=w_codes[:, g * NC : (g + 1) * NC].bitcast(FP8X4),
-                rhs_scale=w_scales[:, g * NC : (g + 1) * NC],
-                start=(g == 0),
-                stop=(g == PASSES - 1),
-            )
 
         new = keep.tile([P, NS, SS, CS], F32)
-        for n in range(NS):
-            pa = act[:, n * NA + 0 : n * NA + 1]
-            po = act[:, n * NA + 1 : n * NA + 2]
-            no = act[:, n * NA + 2 : n * NA + 3]
-            nc.scalar.activation(out=new[:, n], in_=old[:, n], func=ACT.Copy, scale=no)
-            nc.vector.scalar_tensor_tensor(
-                out=new[:, n, 1:SS],
-                in0=old[:, n, 0 : SS - 1],
-                scalar=pa,
-                in1=new[:, n, 1:SS],
-                op0=ALU.mult,
-                op1=ALU.add,
-            )
-            nc.vector.scalar_tensor_tensor(
-                out=new[:, n, 0 : SS - 1],
-                in0=old[:, n, 1:SS],
-                scalar=po,
-                in1=new[:, n, 0 : SS - 1],
-                op0=ALU.mult,
-                op1=ALU.add,
-            )
-            nc.sync.dma_start(out=out[:, n, 1:SS, :], in_=new[:, n, 1:SS, :])
 
-        pushed = keep.tile([P, NC], F32)
-        nc.vector.tensor_tensor(out=pushed[:], in0=push[:], in1=bias[:], op=ALU.add)
+        def keep_term(n):
+            for first in (0, HALF):
+                nc.scalar.activation(
+                    out=new[:, n, first : first + HALF],
+                    in_=old[:, n, first : first + HALF],
+                    func=ACT.Copy,
+                    scale=act[:, n, 2:3],
+                )
+
+        def add_term(n, first, last, shift, action):
+            nc.vector.scalar_tensor_tensor(
+                out=new[:, n, first:last],
+                in0=old[:, n, first + shift : last + shift],
+                scalar=act[:, n, action : action + 1],
+                in1=new[:, n, first:last],
+                op0=ALU.mult,
+                op1=ALU.add,
+            )
+
+        def neighbour_terms(n):
+            add_term(n, 1, HALF, -1, 0)
+            add_term(n, HALF, SS, -1, 0)
+            add_term(n, 0, HALF, 1, 1)
+            nc.sync.dma_start(out=out[:, n, 1:HALF, :], in_=new[:, n, 1:HALF, :])
+            add_term(n, HALF, SS - 1, 1, 1)
+            nc.sync.dma_start(out=out[:, n, HALF:SS, :], in_=new[:, n, HALF:SS, :])
+
+        keep_term(0)
+        keep_term(1)
+        neighbour_terms(0)
+        neighbour_terms(1)
+
+        def regroup(rows, name):
+            bank = psum.tile([P, PASSES, PAIRS, P], F32, name="bank_" + name)
+            words = rows.bitcast(F32)
+            for g in range(PASSES):
+                for u in range(PAIRS):
+                    first = (g * PAIRS + u) * P
+                    nc.tensor.transpose(bank[:, g, u, :], words[:, first : first + P], identity[:])
+            grouped = keep.tile([P, PASSES * P * PACK], BF16, align_bytes=64, name="grouped_" + name)
+            nc.scalar.copy(
+                out=grouped[:].bitcast(F32).rearrange("p (g r u) -> p g r u", g=PASSES, u=PAIRS),
+                in_=bank[:].rearrange("p g u r -> p g r u"),
+            )
+            return grouped
+
+        def quantise(grouped, name):
+            codes = keep.tile([P, PASSES, P], U32, align_bytes=64, name="codes_" + name)
+            scales = keep.tile([P, PASSES, P], U8, align_bytes=64, name="scales_" + name)
+            nc.vector.quantize_mx(
+                out=codes[:].rearrange("p g r -> p (g r)").bitcast(FP8X4),
+                scales=scales[:].rearrange("p g r -> p (g r)"),
+                in_=grouped[:],
+            )
+            return codes, scales
+
+        h_grouped = regroup(h_rows[:], "h")
+        w_grouped = [regroup(w_rows[n][:], "w%d" % n) for n in range(NS)]
+        h_codes, h_scales = quantise(h_grouped, "h")
+        w_quantised = [quantise(w_grouped[n], "w%d" % n) for n in range(NS)]
+
+        push_t = psum.tile([P, NS, P], F32)
+        for n in range(NS):
+            w_codes, w_scales = w_quantised[n]
+            for g in range(PASSES):
+                nc.tensor.matmul_mx(
+                    out=push_t[:, n, :],
+                    lhsT=w_codes[:, g, :].bitcast(FP8X4),
+                    lhsT_scale=w_scales[:, g, :],
+                    rhs=h_codes[:, g, :].bitcast(FP8X4),
+                    rhs_scale=h_scales[:, g, :],
+                    start=(g == 0),
+                    stop=(g == PASSES - 1),
+                )
+
+        keep_term(2)
+        keep_term(3)
+        neighbour_terms(2)
+        neighbour_terms(3)
+
+        biased_t = keep.tile([P, NS, P], F32)
+        biased = psum.tile([P, NS, CS], F32)
+        for n in range(NS):
+            nc.scalar.activation(
+                out=biased_t[:, n, :], in_=push_t[:, n, :], func=ACT.Identity, bias=bias_col[:, n : n + 1]
+            )
+        for n in range(NS):
+            nc.tensor.transpose(biased[:, n, :], biased_t[:, n, :], identity[:])
         for n in range(NS):
             nc.vector.scalar_tensor_tensor(
                 out=new[:, n, 0, :],
-                in0=pushed[:, n * CS : (n + 1) * CS],
-                scalar=act[:, n * NA : n * NA + 1],
+                in0=biased[:, n, :],
+                scalar=act[:, n, 0:1],
                 in1=new[:, n, 0, :],
                 op0=ALU.mult,
                 op1=ALU.add,

@@ -36,9 +36,6 @@ def tile_stackrnncore_pa_s_kernel(tc, h, act_logits, stacks, W_push, b_push, out
 
         logits = keep.tile([P, NS * NA], BF16)
         nc.scalar.dma_start(out=logits[:], in_=act_logits)
-        bias_col = keep.tile([P, NS], BF16)
-        with nc.allow_non_contiguous_dma(reason="512 single elements, once"):
-            nc.scalar.dma_start(out=bias_col[:], in_=b_push.rearrange("(n c) -> c n", c=CS))
 
         old = keep.tile([P, NS, SS, CS], BF16)
         h_rows = keep.tile([P, H], BF16)
@@ -50,6 +47,9 @@ def tile_stackrnncore_pa_s_kernel(tc, h, act_logits, stacks, W_push, b_push, out
             nc.sync.dma_start(out=w_rows[n][:], in_=W_push[n * CS : (n + 1) * CS, :])
         nc.sync.dma_start(out=old[:, 2], in_=stacks[:, 2])
         nc.sync.dma_start(out=old[:, 3], in_=stacks[:, 3])
+        bias_col = keep.tile([P, NS], BF16)
+        with nc.allow_non_contiguous_dma(reason="512 single elements, once, behind all else"):
+            nc.sync.dma_start(out=bias_col[:], in_=b_push.rearrange("(n c) -> c n", c=CS))
 
         identity = keep.tile([P, P], F32)
         make_identity(nc, identity[:])
@@ -172,4 +172,4 @@ def tile_stackrnncore_pa_s_kernel(tc, h, act_logits, stacks, W_push, b_push, out
                 op0=ALU.mult,
                 op1=ALU.add,
             )
-        nc.sync.dma_start(out=out[:, :, 0, :], in_=new[:, :, 0, :])
+            nc.sync.dma_start(out=out[:, n, 0, :], in_=new[:, n, 0, :])

@@ -35,7 +35,7 @@ def tile_stackrnncore_pa_s_kernel(tc, h, act_logits, stacks, W_push, b_push, out
         ctx.enter_context(tc.manual_schedule())
 
         logits = keep.tile([P, NS * NA], BF16)
-        nc.scalar.dma_start(out=logits[:], in_=act_logits)
+        nc.sync.dma_start(out=logits[:], in_=act_logits)
 
         old = keep.tile([P, NS, SS, CS], BF16)
         h_rows = keep.tile([P, H], BF16)

@@ -75,14 +75,22 @@ def tile_stackrnncore_pa_s_kernel(tc, h, act_logits, stacks, W_push, b_push, out
 
         new = keep.tile([P, NS, SS, CS], F32)
 
-        def keep_term(n):
-            for first in (0, HALF):
-                nc.scalar.activation(
-                    out=new[:, n, first : first + HALF],
-                    in_=old[:, n, first : first + HALF],
-                    func=ACT.Copy,
-                    scale=act[:, n, 2:3],
-                )
+        nc.vector.tensor_scalar(
+            out=new[:, 0, 0:HALF],
+            in0=old[:, 0, 0:HALF],
+            scalar1=expd[:, 2:3],
+            scalar2=inv_sum[:],
+            op0=ALU.mult,
+            op1=ALU.mult,
+        )
+
+        def keep_term(n, first):
+            nc.scalar.activation(
+                out=new[:, n, first : first + HALF],
+                in_=old[:, n, first : first + HALF],
+                func=ACT.Copy,
+                scale=act[:, n, 2:3],
+            )
 
         def add_term(n, first, last, shift, action):
             nc.vector.scalar_tensor_tensor(
@@ -102,8 +110,9 @@ def tile_stackrnncore_pa_s_kernel(tc, h, act_logits, stacks, W_push, b_push, out
             add_term(n, HALF, SS - 1, 1, 1)
             nc.sync.dma_start(out=out[:, n, HALF:SS, :], in_=new[:, n, HALF:SS, :])
 
-        keep_term(0)
-        keep_term(1)
+        keep_term(0, HALF)
+        keep_term(1, 0)
+        keep_term(1, HALF)
         neighbour_terms(0)
         neighbour_terms(1)
 
@@ -150,8 +159,9 @@ def tile_stackrnncore_pa_s_kernel(tc, h, act_logits, stacks, W_push, b_push, out
                     stop=(g == PASSES - 1),
                 )
 
-        keep_term(2)
-        keep_term(3)
+        for n in (2, 3):
+            keep_term(n, 0)
+            keep_term(n, HALF)
         neighbour_terms(2)
         neighbour_terms(3)
 

@@ -19,6 +19,10 @@ SS = 8
 HALF = SS // 2
 CS = 128
 NA = 3
+PUSH = 0
+POP = 1
+NOOP = 2
+AHEAD = 2
 PACK = 4
 K_PASS = P * PACK
 PASSES = H // K_PASS
@@ -40,24 +44,19 @@ def tile_stackrnncore_pa_s_kernel(tc, h, act_logits, stacks, W_push, b_push, out
         old = keep.tile([P, NS, SS, CS], BF16)
         h_rows = keep.tile([P, H], BF16)
         w_rows = [keep.tile([P, H], BF16, name="w_rows%d" % n) for n in range(NS)]
-        nc.sync.dma_start(out=old[:, 0], in_=stacks[:, 0])
-        nc.sync.dma_start(out=old[:, 1], in_=stacks[:, 1])
+        for n in range(AHEAD):
+            nc.sync.dma_start(out=old[:, n], in_=stacks[:, n])
         nc.sync.dma_start(out=h_rows[:], in_=h)
         for n in range(NS):
             nc.sync.dma_start(out=w_rows[n][:], in_=W_push[n * CS : (n + 1) * CS, :])
-        nc.sync.dma_start(out=old[:, 2], in_=stacks[:, 2])
-        nc.sync.dma_start(out=old[:, 3], in_=stacks[:, 3])
+        for n in range(AHEAD, NS):
+            nc.sync.dma_start(out=old[:, n], in_=stacks[:, n])
         bias_col = keep.tile([P, NS], BF16)
         with nc.allow_non_contiguous_dma(reason="512 single elements, once, behind all else"):
             nc.sync.dma_start(out=bias_col[:], in_=b_push.rearrange("(n c) -> c n", c=CS))
 
         identity = keep.tile([P, P], F32)
         make_identity(nc, identity[:])
-
-        zero = keep.tile([P, 1], F32)
-        nc.vector.memset(zero[:], 0.0)
-        one = keep.tile([P, 1], F32)
-        nc.scalar.activation(out=one[:], in_=zero[:], func=ACT.Exp)
 
         neg_max = keep.tile([P, 1], F32)
         nc.vector.reduce_max(out=neg_max[:], in_=logits[:], axis=AX.X, negate=True)
@@ -78,7 +77,7 @@ def tile_stackrnncore_pa_s_kernel(tc, h, act_logits, stacks, W_push, b_push, out
         nc.vector.tensor_scalar(
             out=new[:, 0, 0:HALF],
             in0=old[:, 0, 0:HALF],
-            scalar1=expd[:, 2:3],
+            scalar1=expd[:, NOOP : NOOP + 1],
             scalar2=inv_sum[:],
             op0=ALU.mult,
             op1=ALU.mult,
@@ -89,7 +88,7 @@ def tile_stackrnncore_pa_s_kernel(tc, h, act_logits, stacks, W_push, b_push, out
                 out=new[:, n, first : first + HALF],
                 in_=old[:, n, first : first + HALF],
                 func=ACT.Copy,
-                scale=act[:, n, 2:3],
+                scale=act[:, n, NOOP : NOOP + 1],
             )
 
         def add_term(n, first, last, shift, action):
@@ -103,27 +102,30 @@ def tile_stackrnncore_pa_s_kernel(tc, h, act_logits, stacks, W_push, b_push, out
             )
 
         def neighbour_terms(n):
-            add_term(n, 1, HALF, -1, 0)
-            add_term(n, HALF, SS, -1, 0)
-            add_term(n, 0, HALF, 1, 1)
+            add_term(n, 1, HALF, -1, PUSH)
+            add_term(n, HALF, SS, -1, PUSH)
+            add_term(n, 0, HALF, 1, POP)
             nc.sync.dma_start(out=out[:, n, 1:HALF, :], in_=new[:, n, 1:HALF, :])
-            add_term(n, HALF, SS - 1, 1, 1)
+            add_term(n, HALF, SS - 1, 1, POP)
             nc.sync.dma_start(out=out[:, n, HALF:SS, :], in_=new[:, n, HALF:SS, :])
 
         keep_term(0, HALF)
-        keep_term(1, 0)
-        keep_term(1, HALF)
-        neighbour_terms(0)
-        neighbour_terms(1)
+        for n in range(1, AHEAD):
+            keep_term(n, 0)
+            keep_term(n, HALF)
+        for n in range(AHEAD):
+            neighbour_terms(n)
 
         def regroup(rows, name):
             bank = psum.tile([P, PASSES, PAIRS, P], F32, name="bank_" + name)
             words = rows.bitcast(F32)
             for g in range(PASSES):
                 for u in range(PAIRS):
-                    first = (g * PAIRS + u) * P
-                    nc.tensor.transpose(bank[:, g, u, :], words[:, first : first + P], identity[:])
-            grouped = keep.tile([P, PASSES * P * PACK], BF16, align_bytes=64, name="grouped_" + name)
+                    block = (g * PAIRS + u) * P
+                    nc.tensor.transpose(bank[:, g, u, :], words[:, block : block + P], identity[:])
+            grouped = keep.tile(
+                [P, PASSES * P * PACK], BF16, align_bytes=64, name="grouped_" + name
+            )
             nc.scalar.copy(
                 out=grouped[:].bitcast(F32).rearrange("p (g r u) -> p g r u", g=PASSES, u=PAIRS),
                 in_=bank[:].rearrange("p g u r -> p g r u"),
@@ -159,17 +161,20 @@ def tile_stackrnncore_pa_s_kernel(tc, h, act_logits, stacks, W_push, b_push, out
                     stop=(g == PASSES - 1),
                 )
 
-        for n in (2, 3):
+        for n in range(AHEAD, NS):
             keep_term(n, 0)
             keep_term(n, HALF)
-        neighbour_terms(2)
-        neighbour_terms(3)
+        for n in range(AHEAD, NS):
+            neighbour_terms(n)
 
         biased_t = keep.tile([P, NS, P], F32)
         biased = psum.tile([P, NS, CS], F32)
         for n in range(NS):
             nc.scalar.activation(
-                out=biased_t[:, n, :], in_=push_t[:, n, :], func=ACT.Identity, bias=bias_col[:, n : n + 1]
+                out=biased_t[:, n, :],
+                in_=push_t[:, n, :],
+                func=ACT.Identity,
+                bias=bias_col[:, n : n + 1],
             )
         for n in range(NS):
             nc.tensor.transpose(biased[:, n, :], biased_t[:, n, :], identity[:])
@@ -177,7 +182,7 @@ def tile_stackrnncore_pa_s_kernel(tc, h, act_logits, stacks, W_push, b_push, out
             nc.vector.scalar_tensor_tensor(
                 out=new[:, n, 0, :],
                 in0=biased[:, n, :],
-                scalar=act[:, n, 0:1],
+                scalar=act[:, n, PUSH : PUSH + 1],
                 in1=new[:, n, 0, :],
                 op0=ALU.mult,
                 op1=ALU.add,

from contextlib import ExitStack

import concourse.mybir as mybir
from concourse.masks import make_identity

F32 = mybir.dt.float32
BF16 = mybir.dt.bfloat16
U32 = mybir.dt.uint32
U8 = mybir.dt.uint8
FP8X4 = mybir.dt.float8_e4m3fn_x4
ACT = mybir.ActivationFunctionType
ALU = mybir.AluOpType
AX = mybir.AxisListType

P = 128
H = 1024
NS = 4
SS = 8
HALF = SS // 2
CS = 128
NA = 3
PUSH = 0
POP = 1
NOOP = 2
AHEAD = 2
PACK = 4
K_PASS = P * PACK
PASSES = H // K_PASS
PAIRS = 2

FLOPS = 2 * P * H * NS * CS


def tile_stackrnncore_pa_s_kernel(tc, h, act_logits, stacks, W_push, b_push, out):
    nc = tc.nc
    with ExitStack() as ctx:
        keep = ctx.enter_context(tc.tile_pool(name="keep", bufs=1))
        psum = ctx.enter_context(tc.psum_pool(name="psum", bufs=1))
        ctx.enter_context(tc.manual_schedule())

        logits = keep.tile([P, NS * NA], BF16)
        nc.sync.dma_start(out=logits[:], in_=act_logits)

        old = keep.tile([P, NS, SS, CS], BF16)
        h_rows = keep.tile([P, H], BF16)
        w_rows = [keep.tile([P, H], BF16, name="w_rows%d" % n) for n in range(NS)]
        for n in range(AHEAD):
            nc.sync.dma_start(out=old[:, n], in_=stacks[:, n])
        nc.sync.dma_start(out=h_rows[:], in_=h)
        for n in range(NS):
            nc.sync.dma_start(out=w_rows[n][:], in_=W_push[n * CS : (n + 1) * CS, :])
        for n in range(AHEAD, NS):
            nc.sync.dma_start(out=old[:, n], in_=stacks[:, n])
        bias_col = keep.tile([P, NS], BF16)
        with nc.allow_non_contiguous_dma(reason="512 single elements, once, behind all else"):
            nc.sync.dma_start(out=bias_col[:], in_=b_push.rearrange("(n c) -> c n", c=CS))

        identity = keep.tile([P, P], F32)
        make_identity(nc, identity[:])

        neg_max = keep.tile([P, 1], F32)
        nc.vector.reduce_max(out=neg_max[:], in_=logits[:], axis=AX.X, negate=True)
        expd = keep.tile([P, NS * NA], F32)
        exp_sum = keep.tile([P, 1], F32)
        nc.scalar.activation(
            out=expd[:], in_=logits[:], func=ACT.Exp, bias=neg_max[:], accum_out=exp_sum[:]
        )
        inv_sum = keep.tile([P, 1], F32)
        nc.vector.reciprocal(out=inv_sum[:], in_=exp_sum[:])
        act = keep.tile([P, NS, NA], F32)
        nc.vector.tensor_scalar_mul(
            out=act[:].rearrange("p n a -> p (n a)"), in0=expd[:], scalar1=inv_sum[:]
        )

        new = keep.tile([P, NS, SS, CS], F32)

        nc.vector.tensor_scalar(
            out=new[:, 0, 0:HALF],
            in0=old[:, 0, 0:HALF],
            scalar1=expd[:, NOOP : NOOP + 1],
            scalar2=inv_sum[:],
            op0=ALU.mult,
            op1=ALU.mult,
        )

        def keep_term(n, first):
            nc.scalar.activation(
                out=new[:, n, first : first + HALF],
                in_=old[:, n, first : first + HALF],
                func=ACT.Copy,
                scale=act[:, n, NOOP : NOOP + 1],
            )

        def add_term(n, first, last, shift, action):
            nc.vector.scalar_tensor_tensor(
                out=new[:, n, first:last],
                in0=old[:, n, first + shift : last + shift],
                scalar=act[:, n, action : action + 1],
                in1=new[:, n, first:last],
                op0=ALU.mult,
                op1=ALU.add,
            )

        def neighbour_terms(n):
            add_term(n, 1, HALF, -1, PUSH)
            add_term(n, HALF, SS, -1, PUSH)
            add_term(n, 0, HALF, 1, POP)
            nc.sync.dma_start(out=out[:, n, 1:HALF, :], in_=new[:, n, 1:HALF, :])
            add_term(n, HALF, SS - 1, 1, POP)
            nc.sync.dma_start(out=out[:, n, HALF:SS, :], in_=new[:, n, HALF:SS, :])

        keep_term(0, HALF)
        for n in range(1, AHEAD):
            keep_term(n, 0)
            keep_term(n, HALF)
        for n in range(AHEAD):
            neighbour_terms(n)

        def regroup(rows, name):
            bank = psum.tile([P, PASSES, PAIRS, P], F32, name="bank_" + name)
            words = rows.bitcast(F32)
            for g in range(PASSES):
                for u in range(PAIRS):
                    block = (g * PAIRS + u) * P
                    nc.tensor.transpose(bank[:, g, u, :], words[:, block : block + P], identity[:])
            grouped = keep.tile(
                [P, PASSES * P * PACK], BF16, align_bytes=64, name="grouped_" + name
            )
            nc.scalar.copy(
                out=grouped[:].bitcast(F32).rearrange("p (g r u) -> p g r u", g=PASSES, u=PAIRS),
                in_=bank[:].rearrange("p g u r -> p g r u"),
            )
            return grouped

        def quantise(grouped, name):
            codes = keep.tile([P, PASSES, P], U32, align_bytes=64, name="codes_" + name)
            scales = keep.tile([P, PASSES, P], U8, align_bytes=64, name="scales_" + name)
            nc.vector.quantize_mx(
                out=codes[:].rearrange("p g r -> p (g r)").bitcast(FP8X4),
                scales=scales[:].rearrange("p g r -> p (g r)"),
                in_=grouped[:],
            )
            return codes, scales

        h_grouped = regroup(h_rows[:], "h")
        w_grouped = [regroup(w_rows[n][:], "w%d" % n) for n in range(NS)]
        h_codes, h_scales = quantise(h_grouped, "h")
        w_quantised = [quantise(w_grouped[n], "w%d" % n) for n in range(NS)]

        push_t = psum.tile([P, NS, P], F32)
        for n in range(NS):
            w_codes, w_scales = w_quantised[n]
            for g in range(PASSES):
                nc.tensor.matmul_mx(
                    out=push_t[:, n, :],
                    lhsT=w_codes[:, g, :].bitcast(FP8X4),
                    lhsT_scale=w_scales[:, g, :],
                    rhs=h_codes[:, g, :].bitcast(FP8X4),
                    rhs_scale=h_scales[:, g, :],
                    start=(g == 0),
                    stop=(g == PASSES - 1),
                )

        for n in range(AHEAD, NS):
            keep_term(n, 0)
            keep_term(n, HALF)
        for n in range(AHEAD, NS):
            neighbour_terms(n)

        biased_t = keep.tile([P, NS, P], F32)
        biased = psum.tile([P, NS, CS], F32)
        for n in range(NS):
            nc.scalar.activation(
                out=biased_t[:, n, :],
                in_=push_t[:, n, :],
                func=ACT.Identity,
                bias=bias_col[:, n : n + 1],
            )
        for n in range(NS):
            nc.tensor.transpose(biased[:, n, :], biased_t[:, n, :], identity[:])
        for n in range(NS):
            nc.vector.scalar_tensor_tensor(
                out=new[:, n, 0, :],
                in0=biased[:, n, :],
                scalar=act[:, n, PUSH : PUSH + 1],
                in1=new[:, n, 0, :],
                op0=ALU.mult,
                op1=ALU.add,
            )
            nc.sync.dma_start(out=out[:, n, 0, :], in_=new[:, n, 0, :])
